import numpy as np
import ml_dtypes


def mxq(x, axis, fmt="e4m3"):
    dtype, down = {"e4m3": (ml_dtypes.float8_e4m3fn, 7), "e5m2": (ml_dtypes.float8_e5m2, 14)}[fmt]
    v = np.moveaxis(np.asarray(x, np.float32).astype(ml_dtypes.bfloat16).astype(np.float64), axis, -1)
    blocks = v.reshape(v.shape[:-1] + (-1, 32))
    amax = np.abs(blocks).max(-1, keepdims=True)
    byte = np.maximum(np.where(amax > 0, np.frexp(amax)[1] - 1 + 127, 0) - down, 1)
    scale = np.exp2(byte - 127.0)
    codes = (blocks / scale).astype(np.float32).astype(dtype).astype(np.float64)
    return np.moveaxis((codes * scale).reshape(v.shape), -1, axis)


WIDE = False


def mx_kscale(k):
    if not WIDE:
        return np.ones(k)
    levels = np.array([10, -10, 5, -5, 0])
    a = np.random.permutation(np.resize(levels, k // 512 * 4)).reshape(k // 512, 4)
    idx = np.arange(k)
    return np.exp2(a[idx // 512, idx % 128 // 32])


BF16 = ml_dtypes.bfloat16


def bf(x):
    return np.asarray(x, np.float32).astype(BF16)


def f64(x):
    return np.asarray(x).astype(np.float64)


B, S, D_IN, D_OUT, R = 2, 256, 1024, 256, 128
LORA_SCALE = 2.0


def setup_inputs():
    s = mx_kscale(D_IN)
    return {"x": bf(np.random.standard_normal((B, S, D_IN)) * s),
            "weight": bf(np.random.standard_normal((D_OUT, D_IN)) * 1.0 / np.sqrt(D_IN) / s),
            "bias": bf(np.random.standard_normal(D_OUT) * 0.5),
            "lora_left": bf(np.random.standard_normal((D_OUT, R)) * 0.5 / np.sqrt(R)),
            "lora_right": bf(np.random.standard_normal((R, D_IN)) * 0.5 / np.sqrt(D_IN) / s)}


def reference(x, weight, bias, lora_left, lora_right):
    w_eff = f64(weight) + LORA_SCALE * (f64(lora_left) @ f64(lora_right))
    return (mxq(f64(x), 2, "e4m3") @ mxq(w_eff, 1, "e4m3").T) + f64(bias)

@@ -1,0 +1,160 @@
+from contextlib import ExitStack
+
+import concourse.mybir as mybir
+from concourse.masks import make_identity
+
+F32 = mybir.dt.float32
+BF16 = mybir.dt.bfloat16
+U32 = mybir.dt.uint32
+U8 = mybir.dt.uint8
+FP8X4 = mybir.dt.float8_e4m3fn_x4
+ALU = mybir.AluOpType
+
+P = 128
+PACK = 4
+K_PASS = P * PACK
+PAIR = 2
+HALVES = PACK // PAIR
+
+TOKENS = 512
+D_IN = 1024
+D_OUT = 256
+RANK = 128
+LORA_SCALE = 2.0
+
+PASSES = D_IN // K_PASS
+TOKEN_TILES = TOKENS // P
+OUT_TILES = D_OUT // P
+
+FLOPS = 2 * TOKENS * D_OUT * D_IN + 2 * D_OUT * RANK * D_IN
+
+
+def tile_loralinear_s_kernel(tc, x, weight, bias, lora_left, lora_right, out):
+    nc = tc.nc
+    x_tiles = x.flatten_outer_dims().rearrange("(p j) i -> p j i", j=TOKEN_TILES)
+    out_tiles = out.flatten_outer_dims().rearrange("(p j) o -> p j o", j=TOKEN_TILES)
+
+    with ExitStack() as ctx:
+        keep = ctx.enter_context(tc.tile_pool(name="keep", bufs=1))
+        x_pool = ctx.enter_context(tc.tile_pool(name="x_pool", bufs=TOKEN_TILES))
+        psum_t = ctx.enter_context(tc.psum_pool(name="psum_t", bufs=3))
+        psum_m = ctx.enter_context(tc.psum_pool(name="psum_m", bufs=5))
+
+        l_sb = keep.tile([P, OUT_TILES, RANK], BF16)
+        nc.sync.dma_start(out=l_sb[:], in_=lora_left.rearrange("(h p) r -> p h r", p=P))
+        r_sb = keep.tile([P, D_IN], BF16)
+        nc.sync.dma_start(out=r_sb[:], in_=lora_right)
+        w_sb = keep.tile([P, OUT_TILES * D_IN], BF16)
+        nc.sync.dma_start(
+            out=w_sb[:].rearrange("p (h i) -> p h i", h=OUT_TILES),
+            in_=weight.rearrange("(h p) i -> p h i", p=P),
+        )
+        x_sb = []
+        for j in range(TOKEN_TILES):
+            x_j = x_pool.tile([P, D_IN], BF16, name="x_j")
+            nc.sync.dma_start(out=x_j[:], in_=x_tiles[:, j, :])
+            x_sb.append(x_j)
+
+        ident_bf16 = keep.tile([P, P], BF16)
+        make_identity(nc, ident_bf16[:])
+        ident_f32 = keep.tile([P, P], F32)
+        make_identity(nc, ident_f32[:])
+        ones = keep.tile([P, P], BF16)
+        nc.vector.memset(ones[:], 1.0)
+        bias_rows = keep.tile([P, D_OUT], BF16)
+        nc.vector.memset(bias_rows[:], 0.0)
+        nc.scalar.dma_start(out=bias_rows[0:1, :], in_=bias.unsqueeze(0))
+
+        lt_ps = psum_t.tile([P, D_OUT], BF16, tag="t")
+        for h in range(OUT_TILES):
+            nc.tensor.transpose(lt_ps[:, h * P : (h + 1) * P], l_sb[:, h, :], ident_bf16[:])
+        lT_sb = keep.tile([P, D_OUT], BF16)
+        nc.vector.tensor_copy(out=lT_sb[:], in_=lt_ps[:])
+
+        bias_ps = psum_m.tile([P, D_OUT], F32, tag="m")
+        nc.tensor.matmul(bias_ps[:], lhsT=ones[:], rhs=bias_rows[:], start=True, stop=True)
+        bias_sb = keep.tile([P, D_OUT], F32)
+        nc.scalar.copy(out=bias_sb[:], in_=bias_ps[:])
+
+        w_words = w_sb[:].bitcast(F32)
+        wT = keep.tile([P, PASSES * D_OUT * PACK], BF16)
+        wT_words = wT[:].bitcast(F32).rearrange("p (g o u) -> p g o u", g=PASSES, u=HALVES)
+        wT_vals = wT[:].rearrange("p (g o t) -> p g o t", g=PASSES, t=PACK)
+        for g in range(PASSES):
+            wt_ps = psum_t.tile([P, HALVES, D_OUT], F32, tag="t")
+            for u in range(HALVES):
+                for h in range(OUT_TILES):
+                    col = ((h * PASSES + g) * HALVES + u) * P
+                    nc.tensor.transpose(
+                        wt_ps[:, u, h * P : (h + 1) * P], w_words[:, col : col + P], ident_f32[:]
+                    )
+            if g % 2 == 0:
+                nc.vector.tensor_copy(out=wT_words[:, g], in_=wt_ps[:].rearrange("p u o -> p o u"))
+            else:
+                nc.scalar.copy(out=wT_words[:, g], in_=wt_ps[:].rearrange("p u o -> p o u"))
+
+        r_cols = r_sb[:].rearrange("r (g u q e) -> r g u e q", g=PASSES, u=HALVES, e=PAIR)
+        w_grouped = keep.tile([P, PASSES * D_OUT * PACK], BF16, align_bytes=64)
+        w_grouped_vals = w_grouped[:].rearrange("p (g o t) -> p g o t", g=PASSES, t=PACK)
+        w_codes = keep.tile([P, PASSES, D_OUT], U32, align_bytes=64)
+        w_scales = keep.tile([P, PASSES, D_OUT], U8, align_bytes=64)
+        for g in range(PASSES):
+            for h in range(OUT_TILES):
+                o_cols = slice(h * P, (h + 1) * P)
+                d_ps = psum_m.tile([P, PACK, P], F32, tag="m")
+                for u in range(HALVES):
+                    for e in range(PAIR):
+                        nc.tensor.matmul(
+                            d_ps[:, PAIR * u + e, :],
+                            lhsT=r_cols[:, g, u, e, :],
+                            rhs=lT_sb[:, o_cols],
+                            start=True,
+                            stop=True,
+                        )
+                nc.vector.scalar_tensor_tensor(
+                    out=w_grouped_vals[:, g, o_cols, :],
+                    in0=d_ps[:].rearrange("p t o -> p o t"),
+                    scalar=LORA_SCALE,
+                    in1=wT_vals[:, g, o_cols, :],
+                    op0=ALU.mult,
+                    op1=ALU.add,
+                )
+        for g in range(PASSES):
+            nc.vector.quantize_mx(
+                out=w_codes[:, g, :].bitcast(FP8X4),
+                scales=w_scales[:, g, :],
+                in_=w_grouped[:, g * D_OUT * PACK : (g + 1) * D_OUT * PACK],
+            )
+
+        x_codes = keep.tile([P, TOKEN_TILES, PASSES * P], U32, align_bytes=64)
+        x_scales = keep.tile([P, TOKEN_TILES, PASSES * P], U8, align_bytes=64)
+        for j in range(TOKEN_TILES):
+            x_words = x_sb[j][:].bitcast(F32)
+            xt_ps = psum_t.tile([P, PASSES * HALVES, P], F32, tag="t")
+            for c in range(PASSES * HALVES):
+                nc.tensor.transpose(xt_ps[:, c, :], x_words[:, c * P : (c + 1) * P], ident_f32[:])
+            x_grouped = x_pool.tile([P, PASSES * P * PACK], BF16, align_bytes=64)
+            nc.scalar.copy(
+                out=x_grouped[:].bitcast(F32).rearrange("p (g m u) -> p g m u", g=PASSES, u=HALVES),
+                in_=xt_ps[:].rearrange("p (g u) m -> p g m u", u=HALVES),
+            )
+            nc.vector.quantize_mx(
+                out=x_codes[:, j, :].bitcast(FP8X4), scales=x_scales[:, j, :], in_=x_grouped[:]
+            )
+
+        out_sb = keep.tile([P, TOKEN_TILES, D_OUT], F32)
+        for j in range(TOKEN_TILES):
+            acc = psum_m.tile([P, D_OUT], F32, tag="m")
+            for g in range(PASSES):
+                m_cols = slice(g * P, (g + 1) * P)
+                nc.tensor.matmul_mx(
+                    out=acc[:],
+                    lhsT=x_codes[:, j, m_cols].bitcast(FP8X4),
+                    lhsT_scale=x_scales[:, j, m_cols],
+                    rhs=w_codes[:, g, :].bitcast(FP8X4),
+                    rhs_scale=w_scales[:, g, :],
+                    start=(g == 0),
+                    stop=(g == PASSES - 1),
+                )
+            nc.vector.tensor_tensor(out=out_sb[:, j, :], in0=acc[:], in1=bias_sb[:], op=ALU.add)
+            nc.sync.dma_start(out=out_tiles[:, j, :], in_=out_sb[:, j, :])

@@ -23,8 +23,11 @@ RANK = 128
 LORA_SCALE = 2.0
 
 PASSES = D_IN // K_PASS
-TOKEN_TILES = TOKENS // P
 OUT_TILES = D_OUT // P
+TOKEN_TILES = TOKENS // P
+X_LOADS = 2
+TILES_PER_LOAD = TOKEN_TILES // X_LOADS
+LAG = 2
 
 FLOPS = 2 * TOKENS * D_OUT * D_IN + 2 * D_OUT * RANK * D_IN
 
@@ -36,24 +39,36 @@ def tile_loralinear_s_kernel(tc, x, weight, bias, lora_left, lora_right, out):
 
     with ExitStack() as ctx:
         keep = ctx.enter_context(tc.tile_pool(name="keep", bufs=1))
-        x_pool = ctx.enter_context(tc.tile_pool(name="x_pool", bufs=TOKEN_TILES))
+        per_pass = ctx.enter_context(tc.tile_pool(name="per_pass", bufs=PASSES))
+        per_load = ctx.enter_context(tc.tile_pool(name="per_load", bufs=X_LOADS))
+        per_tile = ctx.enter_context(tc.tile_pool(name="per_tile", bufs=TOKEN_TILES))
         psum_t = ctx.enter_context(tc.psum_pool(name="psum_t", bufs=3))
         psum_m = ctx.enter_context(tc.psum_pool(name="psum_m", bufs=5))
+        ctx.enter_context(tc.manual_schedule())
 
         l_sb = keep.tile([P, OUT_TILES, RANK], BF16)
         nc.sync.dma_start(out=l_sb[:], in_=lora_left.rearrange("(h p) r -> p h r", p=P))
-        r_sb = keep.tile([P, D_IN], BF16)
-        nc.sync.dma_start(out=r_sb[:], in_=lora_right)
-        w_sb = keep.tile([P, OUT_TILES * D_IN], BF16)
-        nc.sync.dma_start(
-            out=w_sb[:].rearrange("p (h i) -> p h i", h=OUT_TILES),
-            in_=weight.rearrange("(h p) i -> p h i", p=P),
-        )
+        w_sb = []
+        r_sb = []
+        for g in range(PASSES):
+            i_cols = slice(g * K_PASS, (g + 1) * K_PASS)
+            w_g = per_pass.tile([P, OUT_TILES * K_PASS], BF16, name="w_g")
+            nc.sync.dma_start(
+                out=w_g[:].rearrange("p (h i) -> p h i", h=OUT_TILES),
+                in_=weight[:, i_cols].rearrange("(h p) i -> p h i", p=P),
+            )
+            w_sb.append(w_g)
+            r_g = per_pass.tile([P, K_PASS], BF16, name="r_g")
+            nc.sync.dma_start(out=r_g[:], in_=lora_right[:, i_cols])
+            r_sb.append(r_g)
         x_sb = []
-        for j in range(TOKEN_TILES):
-            x_j = x_pool.tile([P, D_IN], BF16, name="x_j")
-            nc.sync.dma_start(out=x_j[:], in_=x_tiles[:, j, :])
-            x_sb.append(x_j)
+        for a in range(X_LOADS):
+            x_a = per_load.tile([P, TILES_PER_LOAD * D_IN], BF16, name="x_a")
+            nc.sync.dma_start(
+                out=x_a[:].rearrange("p (b i) -> p b i", b=TILES_PER_LOAD),
+                in_=x_tiles[:, a * TILES_PER_LOAD : (a + 1) * TILES_PER_LOAD, :],
+            )
+            x_sb.append(x_a)
 
         ident_bf16 = keep.tile([P, P], BF16)
         make_identity(nc, ident_bf16[:])
@@ -71,34 +86,35 @@ def tile_loralinear_s_kernel(tc, x, weight, bias, lora_left, lora_right, out):
         lT_sb = keep.tile([P, D_OUT], BF16)
         nc.vector.tensor_copy(out=lT_sb[:], in_=lt_ps[:])
 
-        bias_ps = psum_m.tile([P, D_OUT], F32, tag="m")
-        nc.tensor.matmul(bias_ps[:], lhsT=ones[:], rhs=bias_rows[:], start=True, stop=True)
-        bias_sb = keep.tile([P, D_OUT], F32)
-        nc.scalar.copy(out=bias_sb[:], in_=bias_ps[:])
+        w_codes = keep.tile([P, PASSES, D_OUT], U32, align_bytes=64)
+        w_scales = keep.tile([P, PASSES, D_OUT], U8, align_bytes=64)
+        w_grouped = []
 
-        w_words = w_sb[:].bitcast(F32)
-        wT = keep.tile([P, PASSES * D_OUT * PACK], BF16)
-        wT_words = wT[:].bitcast(F32).rearrange("p (g o u) -> p g o u", g=PASSES, u=HALVES)
-        wT_vals = wT[:].rearrange("p (g o t) -> p g o t", g=PASSES, t=PACK)
+        def quantise_w(g):
+            nc.vector.quantize_mx(
+                out=w_codes[:, g, :].bitcast(FP8X4), scales=w_scales[:, g, :], in_=w_grouped[g][:]
+            )
+
         for g in range(PASSES):
+            w_words = w_sb[g][:].bitcast(F32)
             wt_ps = psum_t.tile([P, HALVES, D_OUT], F32, tag="t")
             for u in range(HALVES):
                 for h in range(OUT_TILES):
-                    col = ((h * PASSES + g) * HALVES + u) * P
+                    col = (h * HALVES + u) * P
                     nc.tensor.transpose(
                         wt_ps[:, u, h * P : (h + 1) * P], w_words[:, col : col + P], ident_f32[:]
                     )
-            if g % 2 == 0:
-                nc.vector.tensor_copy(out=wT_words[:, g], in_=wt_ps[:].rearrange("p u o -> p o u"))
+            wT = per_pass.tile([P, D_OUT * PACK], BF16, name="wT")
+            wT_words = wT[:].bitcast(F32).rearrange("p (o u) -> p o u", u=HALVES)
+            if g == 0:
+                nc.vector.tensor_copy(out=wT_words, in_=wt_ps[:].rearrange("p u o -> p o u"))
             else:
-                nc.scalar.copy(out=wT_words[:, g], in_=wt_ps[:].rearrange("p u o -> p o u"))
-
-        r_cols = r_sb[:].rearrange("r (g u q e) -> r g u e q", g=PASSES, u=HALVES, e=PAIR)
-        w_grouped = keep.tile([P, PASSES * D_OUT * PACK], BF16, align_bytes=64)
-        w_grouped_vals = w_grouped[:].rearrange("p (g o t) -> p g o t", g=PASSES, t=PACK)
-        w_codes = keep.tile([P, PASSES, D_OUT], U32, align_bytes=64)
-        w_scales = keep.tile([P, PASSES, D_OUT], U8, align_bytes=64)
-        for g in range(PASSES):
+                nc.scalar.copy(out=wT_words, in_=wt_ps[:].rearrange("p u o -> p o u"))
+            wT_vals = wT[:].rearrange("p (o t) -> p o t", t=PACK)
+            r_cols = r_sb[g][:].rearrange("r (u q e) -> r u e q", u=HALVES, e=PAIR)
+            w_gr = per_pass.tile([P, D_OUT * PACK], BF16, name="w_gr", align_bytes=64)
+            w_gr_vals = w_gr[:].rearrange("p (o t) -> p o t", t=PACK)
+            w_grouped.append(w_gr)
             for h in range(OUT_TILES):
                 o_cols = slice(h * P, (h + 1) * P)
                 d_ps = psum_m.tile([P, PACK, P], F32, tag="m")
@@ -106,45 +122,53 @@ def tile_loralinear_s_kernel(tc, x, weight, bias, lora_left, lora_right, out):
                     for e in range(PAIR):
                         nc.tensor.matmul(
                             d_ps[:, PAIR * u + e, :],
-                            lhsT=r_cols[:, g, u, e, :],
+                            lhsT=r_cols[:, u, e, :],
                             rhs=lT_sb[:, o_cols],
                             start=True,
                             stop=True,
                         )
                 nc.vector.scalar_tensor_tensor(
-                    out=w_grouped_vals[:, g, o_cols, :],
+                    out=w_gr_vals[:, o_cols, :],
                     in0=d_ps[:].rearrange("p t o -> p o t"),
                     scalar=LORA_SCALE,
-                    in1=wT_vals[:, g, o_cols, :],
+                    in1=wT_vals[:, o_cols, :],
                     op0=ALU.mult,
                     op1=ALU.add,
                 )
-        for g in range(PASSES):
-            nc.vector.quantize_mx(
-                out=w_codes[:, g, :].bitcast(FP8X4),
-                scales=w_scales[:, g, :],
-                in_=w_grouped[:, g * D_OUT * PACK : (g + 1) * D_OUT * PACK],
+                if g == 1 and h == 0:
+                    quantise_w(0)
+
+        bias_ps = psum_m.tile([P, D_OUT], F32, tag="m")
+        nc.tensor.matmul(bias_ps[:], lhsT=ones[:], rhs=bias_rows[:], start=True, stop=True)
+        bias_sb = keep.tile([P, D_OUT], F32)
+        nc.scalar.copy(out=bias_sb[:], in_=bias_ps[:])
+
+        x_grouped = []
+        for j in range(TOKEN_TILES):
+            x_words = x_sb[j // TILES_PER_LOAD][:].bitcast(F32)
+            xt_ps = psum_t.tile([P, PASSES * HALVES, P], F32, tag="t")
+            for c in range(PASSES * HALVES):
+                col = ((j % TILES_PER_LOAD) * PASSES * HALVES + c) * P
+                nc.tensor.transpose(xt_ps[:, c, :], x_words[:, col : col + P], ident_f32[:])
+            x_gr = per_tile.tile([P, PASSES * P * PACK], BF16, name="x_gr", align_bytes=64)
+            nc.scalar.copy(
+                out=x_gr[:].bitcast(F32).rearrange("p (g m u) -> p g m u", g=PASSES, u=HALVES),
+                in_=xt_ps[:].rearrange("p (g u) m -> p g m u", u=HALVES),
             )
+            x_grouped.append(x_gr)
 
         x_codes = keep.tile([P, TOKEN_TILES, PASSES * P], U32, align_bytes=64)
         x_scales = keep.tile([P, TOKEN_TILES, PASSES * P], U8, align_bytes=64)
-        for j in range(TOKEN_TILES):
-            x_words = x_sb[j][:].bitcast(F32)
-            xt_ps = psum_t.tile([P, PASSES * HALVES, P], F32, tag="t")
-            for c in range(PASSES * HALVES):
-                nc.tensor.transpose(xt_ps[:, c, :], x_words[:, c * P : (c + 1) * P], ident_f32[:])
-            x_grouped = x_pool.tile([P, PASSES * P * PACK], BF16, align_bytes=64)
-            nc.scalar.copy(
-                out=x_grouped[:].bitcast(F32).rearrange("p (g m u) -> p g m u", g=PASSES, u=HALVES),
-                in_=xt_ps[:].rearrange("p (g u) m -> p g m u", u=HALVES),
-            )
-            nc.vector.quantize_mx(
-                out=x_codes[:, j, :].bitcast(FP8X4), scales=x_scales[:, j, :], in_=x_grouped[:]
-            )
-
         out_sb = keep.tile([P, TOKEN_TILES, D_OUT], F32)
-        for j in range(TOKEN_TILES):
-            acc = psum_m.tile([P, D_OUT], F32, tag="m")
+        products = []
+
+        def quantise_and_multiply(j):
+            nc.vector.quantize_mx(
+                out=x_codes[:, j, :].bitcast(FP8X4), scales=x_scales[:, j, :], in_=x_grouped[j][:]
+            )
+            if j == 0:
+                quantise_w(1)
+            acc = psum_m.tile([P, D_OUT], F32, tag="m", name="acc")
             for g in range(PASSES):
                 m_cols = slice(g * P, (g + 1) * P)
                 nc.tensor.matmul_mx(
@@ -156,5 +180,16 @@ def tile_loralinear_s_kernel(tc, x, weight, bias, lora_left, lora_right, out):
                     start=(g == 0),
                     stop=(g == PASSES - 1),
                 )
-            nc.vector.tensor_tensor(out=out_sb[:, j, :], in0=acc[:], in1=bias_sb[:], op=ALU.add)
+            products.append(acc)
+
+        def add_bias_and_store(j):
+            nc.vector.tensor_tensor(
+                out=out_sb[:, j, :], in0=products[j][:], in1=bias_sb[:], op=ALU.add
+            )
             nc.sync.dma_start(out=out_tiles[:, j, :], in_=out_sb[:, j, :])
+
+        for j in range(TOKEN_TILES + LAG):
+            if j < TOKEN_TILES:
+                quantise_and_multiply(j)
+            if j >= LAG:
+                add_bias_and_store(j - LAG)

@@ -25,8 +25,6 @@ LORA_SCALE = 2.0
 PASSES = D_IN // K_PASS
 OUT_TILES = D_OUT // P
 TOKEN_TILES = TOKENS // P
-X_LOADS = 2
-TILES_PER_LOAD = TOKEN_TILES // X_LOADS
 LAG = 2
 
 FLOPS = 2 * TOKENS * D_OUT * D_IN + 2 * D_OUT * RANK * D_IN
@@ -36,11 +34,12 @@ def tile_loralinear_s_kernel(tc, x, weight, bias, lora_left, lora_right, out):
     nc = tc.nc
     x_tiles = x.flatten_outer_dims().rearrange("(p j) i -> p j i", j=TOKEN_TILES)
     out_tiles = out.flatten_outer_dims().rearrange("(p j) o -> p j o", j=TOKEN_TILES)
+    blocks = [(g, h) for g in range(PASSES) for h in range(OUT_TILES)]
 
     with ExitStack() as ctx:
         keep = ctx.enter_context(tc.tile_pool(name="keep", bufs=1))
         per_pass = ctx.enter_context(tc.tile_pool(name="per_pass", bufs=PASSES))
-        per_load = ctx.enter_context(tc.tile_pool(name="per_load", bufs=X_LOADS))
+        per_block = ctx.enter_context(tc.tile_pool(name="per_block", bufs=len(blocks)))
         per_tile = ctx.enter_context(tc.tile_pool(name="per_tile", bufs=TOKEN_TILES))
         psum_t = ctx.enter_context(tc.psum_pool(name="psum_t", bufs=3))
         psum_m = ctx.enter_context(tc.psum_pool(name="psum_m", bufs=5))
@@ -50,25 +49,20 @@ def tile_loralinear_s_kernel(tc, x, weight, bias, lora_left, lora_right, out):
         nc.sync.dma_start(out=l_sb[:], in_=lora_left.rearrange("(h p) r -> p h r", p=P))
         w_sb = []
         r_sb = []
-        for g in range(PASSES):
+        for g, h in blocks:
             i_cols = slice(g * K_PASS, (g + 1) * K_PASS)
-            w_g = per_pass.tile([P, OUT_TILES * K_PASS], BF16, name="w_g")
-            nc.sync.dma_start(
-                out=w_g[:].rearrange("p (h i) -> p h i", h=OUT_TILES),
-                in_=weight[:, i_cols].rearrange("(h p) i -> p h i", p=P),
-            )
-            w_sb.append(w_g)
-            r_g = per_pass.tile([P, K_PASS], BF16, name="r_g")
-            nc.sync.dma_start(out=r_g[:], in_=lora_right[:, i_cols])
-            r_sb.append(r_g)
+            w_gh = per_block.tile([P, K_PASS], BF16, name="w_gh")
+            nc.sync.dma_start(out=w_gh[:], in_=weight[h * P : (h + 1) * P, i_cols])
+            w_sb.append(w_gh)
+            if h == 0:
+                r_g = per_pass.tile([P, K_PASS], BF16, name="r_g")
+                nc.sync.dma_start(out=r_g[:], in_=lora_right[:, i_cols])
+                r_sb.append(r_g)
         x_sb = []
-        for a in range(X_LOADS):
-            x_a = per_load.tile([P, TILES_PER_LOAD * D_IN], BF16, name="x_a")
-            nc.sync.dma_start(
-                out=x_a[:].rearrange("p (b i) -> p b i", b=TILES_PER_LOAD),
-                in_=x_tiles[:, a * TILES_PER_LOAD : (a + 1) * TILES_PER_LOAD, :],
-            )
-            x_sb.append(x_a)
+        for j in range(TOKEN_TILES):
+            x_j = per_tile.tile([P, D_IN], BF16, name="x_j")
+            nc.sync.dma_start(out=x_j[:], in_=x_tiles[:, j, :])
+            x_sb.append(x_j)
 
         ident_bf16 = keep.tile([P, P], BF16)
         make_identity(nc, ident_bf16[:])
@@ -84,59 +78,64 @@ def tile_loralinear_s_kernel(tc, x, weight, bias, lora_left, lora_right, out):
         for h in range(OUT_TILES):
             nc.tensor.transpose(lt_ps[:, h * P : (h + 1) * P], l_sb[:, h, :], ident_bf16[:])
         lT_sb = keep.tile([P, D_OUT], BF16)
-        nc.vector.tensor_copy(out=lT_sb[:], in_=lt_ps[:])
+        nc.scalar.copy(out=lT_sb[:], in_=lt_ps[:])
 
         w_codes = keep.tile([P, PASSES, D_OUT], U32, align_bytes=64)
         w_scales = keep.tile([P, PASSES, D_OUT], U8, align_bytes=64)
         w_grouped = []
+        for g in range(PASSES):
+            w_gr = per_pass.tile([P, D_OUT * PACK], BF16, name="w_gr", align_bytes=64)
+            w_grouped.append(w_gr)
+        wT_sb = []
+
+        def transpose_weight(n):
+            w_words = w_sb[n][:].bitcast(F32)
+            wt_ps = psum_t.tile([P, HALVES, P], F32, tag="t", name="wt_ps")
+            for u in range(HALVES):
+                nc.tensor.transpose(wt_ps[:, u, :], w_words[:, u * P : (u + 1) * P], ident_f32[:])
+            wT = per_block.tile([P, P * PACK], BF16, name="wT")
+            wT_words = wT[:].bitcast(F32).rearrange("p (o u) -> p o u", u=HALVES)
+            if n == 0:
+                nc.vector.tensor_copy(out=wT_words, in_=wt_ps[:].rearrange("p u o -> p o u"))
+            else:
+                nc.scalar.copy(out=wT_words, in_=wt_ps[:].rearrange("p u o -> p o u"))
+            wT_sb.append(wT)
+
+        def merge(n):
+            g, h = blocks[n]
+            o_cols = slice(h * P, (h + 1) * P)
+            r_cols = r_sb[g][:].rearrange("r (u q e) -> r u e q", u=HALVES, e=PAIR)
+            d_ps = psum_m.tile([P, PACK, P], F32, tag="m", name="d_ps")
+            for u in range(HALVES):
+                for e in range(PAIR):
+                    nc.tensor.matmul(
+                        d_ps[:, PAIR * u + e, :],
+                        lhsT=r_cols[:, u, e, :],
+                        rhs=lT_sb[:, o_cols],
+                        start=True,
+                        stop=True,
+                    )
+            nc.vector.scalar_tensor_tensor(
+                out=w_grouped[g][:].rearrange("p (o t) -> p o t", t=PACK)[:, o_cols, :],
+                in0=d_ps[:].rearrange("p t o -> p o t"),
+                scalar=LORA_SCALE,
+                in1=wT_sb[n][:].rearrange("p (o t) -> p o t", t=PACK),
+                op0=ALU.mult,
+                op1=ALU.add,
+            )
 
         def quantise_w(g):
             nc.vector.quantize_mx(
                 out=w_codes[:, g, :].bitcast(FP8X4), scales=w_scales[:, g, :], in_=w_grouped[g][:]
             )
 
-        for g in range(PASSES):
-            w_words = w_sb[g][:].bitcast(F32)
-            wt_ps = psum_t.tile([P, HALVES, D_OUT], F32, tag="t")
-            for u in range(HALVES):
-                for h in range(OUT_TILES):
-                    col = (h * HALVES + u) * P
-                    nc.tensor.transpose(
-                        wt_ps[:, u, h * P : (h + 1) * P], w_words[:, col : col + P], ident_f32[:]
-                    )
-            wT = per_pass.tile([P, D_OUT * PACK], BF16, name="wT")
-            wT_words = wT[:].bitcast(F32).rearrange("p (o u) -> p o u", u=HALVES)
-            if g == 0:
-                nc.vector.tensor_copy(out=wT_words, in_=wt_ps[:].rearrange("p u o -> p o u"))
-            else:
-                nc.scalar.copy(out=wT_words, in_=wt_ps[:].rearrange("p u o -> p o u"))
-            wT_vals = wT[:].rearrange("p (o t) -> p o t", t=PACK)
-            r_cols = r_sb[g][:].rearrange("r (u q e) -> r u e q", u=HALVES, e=PAIR)
-            w_gr = per_pass.tile([P, D_OUT * PACK], BF16, name="w_gr", align_bytes=64)
-            w_gr_vals = w_gr[:].rearrange("p (o t) -> p o t", t=PACK)
-            w_grouped.append(w_gr)
-            for h in range(OUT_TILES):
-                o_cols = slice(h * P, (h + 1) * P)
-                d_ps = psum_m.tile([P, PACK, P], F32, tag="m")
-                for u in range(HALVES):
-                    for e in range(PAIR):
-                        nc.tensor.matmul(
-                            d_ps[:, PAIR * u + e, :],
-                            lhsT=r_cols[:, u, e, :],
-                            rhs=lT_sb[:, o_cols],
-                            start=True,
-                            stop=True,
-                        )
-                nc.vector.scalar_tensor_tensor(
-                    out=w_gr_vals[:, o_cols, :],
-                    in0=d_ps[:].rearrange("p t o -> p o t"),
-                    scalar=LORA_SCALE,
-                    in1=wT_vals[:, o_cols, :],
-                    op0=ALU.mult,
-                    op1=ALU.add,
-                )
-                if g == 1 and h == 0:
-                    quantise_w(0)
+        transpose_weight(0)
+        for n in range(len(blocks)):
+            if n + 1 < len(blocks):
+                transpose_weight(n + 1)
+            merge(n)
+            if n == OUT_TILES:
+                quantise_w(0)
 
         bias_ps = psum_m.tile([P, D_OUT], F32, tag="m")
         nc.tensor.matmul(bias_ps[:], lhsT=ones[:], rhs=bias_rows[:], start=True, stop=True)
@@ -145,11 +144,10 @@ def tile_loralinear_s_kernel(tc, x, weight, bias, lora_left, lora_right, out):
 
         x_grouped = []
         for j in range(TOKEN_TILES):
-            x_words = x_sb[j // TILES_PER_LOAD][:].bitcast(F32)
+            x_words = x_sb[j][:].bitcast(F32)
             xt_ps = psum_t.tile([P, PASSES * HALVES, P], F32, tag="t")
             for c in range(PASSES * HALVES):
-                col = ((j % TILES_PER_LOAD) * PASSES * HALVES + c) * P
-                nc.tensor.transpose(xt_ps[:, c, :], x_words[:, col : col + P], ident_f32[:])
+                nc.tensor.transpose(xt_ps[:, c, :], x_words[:, c * P : (c + 1) * P], ident_f32[:])
             x_gr = per_tile.tile([P, PASSES * P * PACK], BF16, name="x_gr", align_bytes=64)
             nc.scalar.copy(
                 out=x_gr[:].bitcast(F32).rearrange("p (g m u) -> p g m u", g=PASSES, u=HALVES),

@@ -129,10 +129,8 @@ def tile_loralinear_s_kernel(tc, x, weight, bias, lora_left, lora_right, out):
                 out=w_codes[:, g, :].bitcast(FP8X4), scales=w_scales[:, g, :], in_=w_grouped[g][:]
             )
 
-        transpose_weight(0)
         for n in range(len(blocks)):
-            if n + 1 < len(blocks):
-                transpose_weight(n + 1)
+            transpose_weight(n)
             merge(n)
             if n == OUT_TILES:
                 quantise_w(0)

from contextlib import ExitStack

import concourse.mybir as mybir
from concourse.masks import make_identity

F32 = mybir.dt.float32
BF16 = mybir.dt.bfloat16
U32 = mybir.dt.uint32
U8 = mybir.dt.uint8
FP8X4 = mybir.dt.float8_e4m3fn_x4
ALU = mybir.AluOpType

P = 128
PACK = 4
K_PASS = P * PACK
PAIR = 2
HALVES = PACK // PAIR

TOKENS = 512
D_IN = 1024
D_OUT = 256
RANK = 128
LORA_SCALE = 2.0

PASSES = D_IN // K_PASS
OUT_TILES = D_OUT // P
TOKEN_TILES = TOKENS // P
LAG = 2

FLOPS = 2 * TOKENS * D_OUT * D_IN + 2 * D_OUT * RANK * D_IN


def tile_loralinear_s_kernel(tc, x, weight, bias, lora_left, lora_right, out):
    nc = tc.nc
    x_tiles = x.flatten_outer_dims().rearrange("(p j) i -> p j i", j=TOKEN_TILES)
    out_tiles = out.flatten_outer_dims().rearrange("(p j) o -> p j o", j=TOKEN_TILES)
    blocks = [(g, h) for g in range(PASSES) for h in range(OUT_TILES)]

    with ExitStack() as ctx:
        keep = ctx.enter_context(tc.tile_pool(name="keep", bufs=1))
        per_pass = ctx.enter_context(tc.tile_pool(name="per_pass", bufs=PASSES))
        per_block = ctx.enter_context(tc.tile_pool(name="per_block", bufs=len(blocks)))
        per_tile = ctx.enter_context(tc.tile_pool(name="per_tile", bufs=TOKEN_TILES))
        psum_t = ctx.enter_context(tc.psum_pool(name="psum_t", bufs=3))
        psum_m = ctx.enter_context(tc.psum_pool(name="psum_m", bufs=5))
        ctx.enter_context(tc.manual_schedule())

        l_sb = keep.tile([P, OUT_TILES, RANK], BF16)
        nc.sync.dma_start(out=l_sb[:], in_=lora_left.rearrange("(h p) r -> p h r", p=P))
        w_sb = []
        r_sb = []
        for g, h in blocks:
            i_cols = slice(g * K_PASS, (g + 1) * K_PASS)
            w_gh = per_block.tile([P, K_PASS], BF16, name="w_gh")
            nc.sync.dma_start(out=w_gh[:], in_=weight[h * P : (h + 1) * P, i_cols])
            w_sb.append(w_gh)
            if h == 0:
                r_g = per_pass.tile([P, K_PASS], BF16, name="r_g")
                nc.sync.dma_start(out=r_g[:], in_=lora_right[:, i_cols])
                r_sb.append(r_g)
        x_sb = []
        for j in range(TOKEN_TILES):
            x_j = per_tile.tile([P, D_IN], BF16, name="x_j")
            nc.sync.dma_start(out=x_j[:], in_=x_tiles[:, j, :])
            x_sb.append(x_j)

        ident_bf16 = keep.tile([P, P], BF16)
        make_identity(nc, ident_bf16[:])
        ident_f32 = keep.tile([P, P], F32)
        make_identity(nc, ident_f32[:])
        ones = keep.tile([P, P], BF16)
        nc.vector.memset(ones[:], 1.0)
        bias_rows = keep.tile([P, D_OUT], BF16)
        nc.vector.memset(bias_rows[:], 0.0)
        nc.scalar.dma_start(out=bias_rows[0:1, :], in_=bias.unsqueeze(0))

        lt_ps = psum_t.tile([P, D_OUT], BF16, tag="t")
        for h in range(OUT_TILES):
            nc.tensor.transpose(lt_ps[:, h * P : (h + 1) * P], l_sb[:, h, :], ident_bf16[:])
        lT_sb = keep.tile([P, D_OUT], BF16)
        nc.scalar.copy(out=lT_sb[:], in_=lt_ps[:])

        w_codes = keep.tile([P, PASSES, D_OUT], U32, align_bytes=64)
        w_scales = keep.tile([P, PASSES, D_OUT], U8, align_bytes=64)
        w_grouped = []
        for g in range(PASSES):
            w_gr = per_pass.tile([P, D_OUT * PACK], BF16, name="w_gr", align_bytes=64)
            w_grouped.append(w_gr)
        wT_sb = []

        def transpose_weight(n):
            w_words = w_sb[n][:].bitcast(F32)
            wt_ps = psum_t.tile([P, HALVES, P], F32, tag="t", name="wt_ps")
            for u in range(HALVES):
                nc.tensor.transpose(wt_ps[:, u, :], w_words[:, u * P : (u + 1) * P], ident_f32[:])
            wT = per_block.tile([P, P * PACK], BF16, name="wT")
            wT_words = wT[:].bitcast(F32).rearrange("p (o u) -> p o u", u=HALVES)
            if n == 0:
                nc.vector.tensor_copy(out=wT_words, in_=wt_ps[:].rearrange("p u o -> p o u"))
            else:
                nc.scalar.copy(out=wT_words, in_=wt_ps[:].rearrange("p u o -> p o u"))
            wT_sb.append(wT)

        def merge(n):
            g, h = blocks[n]
            o_cols = slice(h * P, (h + 1) * P)
            r_cols = r_sb[g][:].rearrange("r (u q e) -> r u e q", u=HALVES, e=PAIR)
            d_ps = psum_m.tile([P, PACK, P], F32, tag="m", name="d_ps")
            for u in range(HALVES):
                for e in range(PAIR):
                    nc.tensor.matmul(
                        d_ps[:, PAIR * u + e, :],
                        lhsT=r_cols[:, u, e, :],
                        rhs=lT_sb[:, o_cols],
                        start=True,
                        stop=True,
                    )
            nc.vector.scalar_tensor_tensor(
                out=w_grouped[g][:].rearrange("p (o t) -> p o t", t=PACK)[:, o_cols, :],
                in0=d_ps[:].rearrange("p t o -> p o t"),
                scalar=LORA_SCALE,
                in1=wT_sb[n][:].rearrange("p (o t) -> p o t", t=PACK),
                op0=ALU.mult,
                op1=ALU.add,
            )

        def quantise_w(g):
            nc.vector.quantize_mx(
                out=w_codes[:, g, :].bitcast(FP8X4), scales=w_scales[:, g, :], in_=w_grouped[g][:]
            )

        for n in range(len(blocks)):
            transpose_weight(n)
            merge(n)
            if n == OUT_TILES:
                quantise_w(0)

        bias_ps = psum_m.tile([P, D_OUT], F32, tag="m")
        nc.tensor.matmul(bias_ps[:], lhsT=ones[:], rhs=bias_rows[:], start=True, stop=True)
        bias_sb = keep.tile([P, D_OUT], F32)
        nc.scalar.copy(out=bias_sb[:], in_=bias_ps[:])

        x_grouped = []
        for j in range(TOKEN_TILES):
            x_words = x_sb[j][:].bitcast(F32)
            xt_ps = psum_t.tile([P, PASSES * HALVES, P], F32, tag="t")
            for c in range(PASSES * HALVES):
                nc.tensor.transpose(xt_ps[:, c, :], x_words[:, c * P : (c + 1) * P], ident_f32[:])
            x_gr = per_tile.tile([P, PASSES * P * PACK], BF16, name="x_gr", align_bytes=64)
            nc.scalar.copy(
                out=x_gr[:].bitcast(F32).rearrange("p (g m u) -> p g m u", g=PASSES, u=HALVES),
                in_=xt_ps[:].rearrange("p (g u) m -> p g m u", u=HALVES),
            )
            x_grouped.append(x_gr)

        x_codes = keep.tile([P, TOKEN_TILES, PASSES * P], U32, align_bytes=64)
        x_scales = keep.tile([P, TOKEN_TILES, PASSES * P], U8, align_bytes=64)
        out_sb = keep.tile([P, TOKEN_TILES, D_OUT], F32)
        products = []

        def quantise_and_multiply(j):
            nc.vector.quantize_mx(
                out=x_codes[:, j, :].bitcast(FP8X4), scales=x_scales[:, j, :], in_=x_grouped[j][:]
            )
            if j == 0:
                quantise_w(1)
            acc = psum_m.tile([P, D_OUT], F32, tag="m", name="acc")
            for g in range(PASSES):
                m_cols = slice(g * P, (g + 1) * P)
                nc.tensor.matmul_mx(
                    out=acc[:],
                    lhsT=x_codes[:, j, m_cols].bitcast(FP8X4),
                    lhsT_scale=x_scales[:, j, m_cols],
                    rhs=w_codes[:, g, :].bitcast(FP8X4),
                    rhs_scale=w_scales[:, g, :],
                    start=(g == 0),
                    stop=(g == PASSES - 1),
                )
            products.append(acc)

        def add_bias_and_store(j):
            nc.vector.tensor_tensor(
                out=out_sb[:, j, :], in0=products[j][:], in1=bias_sb[:], op=ALU.add
            )
            nc.sync.dma_start(out=out_tiles[:, j, :], in_=out_sb[:, j, :])

        for j in range(TOKEN_TILES + LAG):
            if j < TOKEN_TILES:
                quantise_and_multiply(j)
            if j >= LAG:
                add_bias_and_store(j - LAG)
